import numpy as np
import ml_dtypes


def mxq(x, axis, fmt="e4m3"):
    dtype, down = {"e4m3": (ml_dtypes.float8_e4m3fn, 7), "e5m2": (ml_dtypes.float8_e5m2, 14)}[fmt]
    v = np.moveaxis(np.asarray(x, np.float32).astype(ml_dtypes.bfloat16).astype(np.float64), axis, -1)
    blocks = v.reshape(v.shape[:-1] + (-1, 32))
    amax = np.abs(blocks).max(-1, keepdims=True)
    byte = np.maximum(np.where(amax > 0, np.frexp(amax)[1] - 1 + 127, 0) - down, 1)
    scale = np.exp2(byte - 127.0)
    codes = (blocks / scale).astype(np.float32).astype(dtype).astype(np.float64)
    return np.moveaxis((codes * scale).reshape(v.shape), -1, axis)


WIDE = False


def mx_kscale(k):
    if not WIDE:
        return np.ones(k)
    levels = np.array([10, -10, 5, -5, 0])
    a = np.random.permutation(np.resize(levels, k // 512 * 4)).reshape(k // 512, 4)
    idx = np.arange(k)
    return np.exp2(a[idx // 512, idx % 128 // 32])


BF16 = ml_dtypes.bfloat16


def bf(x):
    return np.asarray(x, np.float32).astype(BF16)


def f64(x):
    return np.asarray(x).astype(np.float64)


B, S, D, C, M, H = 4, 1024, 512, 16, 512, 4
LN_EPS = 1e-5


def sigmoid(v):
    return 1.0 / (1.0 + np.exp(-v))


def setup_inputs():
    s = mx_kscale(M)
    t = mx_kscale(M)
    u = mx_kscale(M)
    g = np.concatenate([np.ones(D), u])
    return {
        "x": bf(np.random.standard_normal((B, S, D))),
        "query": bf(np.random.standard_normal((B, S, M)) * u),
        "ctx": bf(np.random.standard_normal((B, S, M)) * 0.5 * s),
        "attn_out_w": bf(np.random.standard_normal((M, M)) * 2.0 / np.sqrt(M) * t[:, None] / s[None, :]),
        "attn_out_b": bf(np.random.standard_normal(M) * 0.3 * t),
        "op_w": bf(np.random.standard_normal((D, M)) / np.sqrt(M) / t[None, :]),
        "op_b": bf(np.random.standard_normal(D) * 0.3 + 0.3),
        "gate_w": bf(np.random.standard_normal((D, D + M)) / np.sqrt(D + M) / g[None, :]),
        "gate_b": bf(np.random.standard_normal(D) * 0.5),
        "ln_g": bf(1.0 + 0.1 * np.random.standard_normal(D)),
        "ln_b": bf(0.1 * np.random.standard_normal(D)),
    }


def reference(x, query, ctx, attn_out_w, attn_out_b, op_w, op_b, gate_w, gate_b, ln_g, ln_b):
    x = f64(x)
    r = (mxq(f64(ctx), 2, "e4m3") @ mxq(f64(attn_out_w), 1, "e4m3").T) + f64(attn_out_b)
    retrieved = (mxq(r, 2, "e4m3") @ mxq(f64(op_w), 1, "e4m3").T) + f64(op_b)
    gate_in = np.concatenate([x, f64(query)], axis=-1)
    gate = sigmoid((mxq(gate_in, 2, "e4m3") @ mxq(f64(gate_w), 1, "e4m3").T) + f64(gate_b))
    y = gate * x + (1.0 - gate) * retrieved
    mu = y.mean(axis=-1, keepdims=True)
    var = y.var(axis=-1, keepdims=True)
    return (y - mu) / np.sqrt(var + LN_EPS) * f64(ln_g) + f64(ln_b)

@@ -1,0 +1,371 @@
+from contextlib import ExitStack
+import math
+
+import concourse.mybir as mybir
+from concourse.masks import make_identity
+
+F32 = mybir.dt.float32
+BF16 = mybir.dt.bfloat16
+U32 = mybir.dt.uint32
+U8 = mybir.dt.uint8
+FP8X4 = mybir.dt.float8_e4m3fn_x4
+ALU = mybir.AluOpType
+ACT = mybir.ActivationFunctionType
+
+P = 128
+TOKENS = 4096
+WIDTH = 512
+GROUP = 512
+N_GROUPS = TOKENS // GROUP
+LN_EPS = 1e-5
+FLOPS = 2 * TOKENS * WIDTH * (512 + 512 + 1024)
+
+MANUAL = True
+
+
+def tile_rotelearningmemory_pa_t_kernel(
+    tc, x, query, ctx, attn_out_w, attn_out_b, op_w, op_b, gate_w, gate_b, ln_g, ln_b, out
+):
+    nc = tc.nc
+    x_rows = x.flatten_outer_dims()
+    q_rows = query.flatten_outer_dims()
+    c_rows = ctx.flatten_outer_dims()
+    o_rows = out.flatten_outer_dims()
+
+    with ExitStack() as stack:
+        if MANUAL:
+            stack.enter_context(tc.manual_schedule())
+        const = stack.enter_context(tc.tile_pool(name="const", bufs=1))
+        wtmp = stack.enter_context(tc.tile_pool(name="wtmp", bufs=2))
+        raws = stack.enter_context(tc.tile_pool(name="raws", bufs=3))
+        grps = stack.enter_context(tc.tile_pool(name="grps", bufs=2))
+        cods = stack.enter_context(tc.tile_pool(name="cods", bufs=2))
+        work = stack.enter_context(tc.tile_pool(name="work", bufs=2))
+        stat = stack.enter_context(tc.tile_pool(name="stat", bufs=3))
+        pv = stack.enter_context(tc.psum_pool(name="pv", bufs=3))
+        ps = stack.enter_context(tc.psum_pool(name="ps", bufs=5))
+
+        identf = const.tile([P, P], F32, name="identf")
+        make_identity(nc, identf[:])
+        identb = const.tile([P, P], BF16, name="identb")
+        make_identity(nc, identb[:])
+        mhalf = const.tile([P, 2], F32, name="mhalf")
+        nc.gpsimd.memset(mhalf[:], -0.5)
+        btile = const.tile([P, 2 * P], BF16, name="btile")
+        nc.vector.memset(btile[:], 0.0)
+        junk = const.tile([P, WIDTH], BF16, name="junk")
+
+        for v, vec in enumerate((attn_out_b, op_b, gate_b)):
+            nc.scalar.dma_start(out=btile[2 * v : 2 * v + 2, :], in_=vec.rearrange("(u w) -> u w", u=2))
+
+        def load_weight(w, cols, name):
+            raw = const.tile([P, 4, cols], BF16, name=name)
+            nc.sync.dma_start(
+                out=raw[:].rearrange("m (u e) k -> m u (e k)", u=2),
+                in_=w.rearrange("(u m e) k -> m u (e k)", u=2, e=2),
+            )
+            return raw
+
+        groups = {}
+
+        def load(g):
+            st = {}
+            groups[g] = st
+            rows = slice(g * GROUP, (g + 1) * GROUP)
+            for key, src, bufs in (("rawc", c_rows, 3), ("rawx", x_rows, 4), ("rawq", q_rows, 3)):
+                raw = raws.tile([P, 4, WIDTH], BF16, name="%s%d" % (key, g), tag=key, bufs=bufs)
+                nc.sync.dma_start(out=raw[:], in_=src[rows, :].rearrange("(p j) k -> p j k", j=4))
+                st[key] = raw
+
+        w1raw = load_weight(attn_out_w, 512, "w1raw")
+        load(0)
+        wgraw = load_weight(gate_w, 1024, "wgraw")
+        w2raw = load_weight(op_w, 512, "w2raw")
+        load(1)
+
+        lng = const.tile([P, WIDTH], BF16, name="lng")
+        nc.scalar.dma_start(out=lng[:], in_=ln_g.partition_broadcast(P))
+        lnb = const.tile([P, WIDTH], BF16, name="lnb")
+        nc.scalar.dma_start(out=lnb[:], in_=ln_b.partition_broadcast(P))
+        lngs = const.tile([P, WIDTH], F32, name="lngs")
+        nc.gpsimd.tensor_scalar(
+            out=lngs[:], in0=lng[:], scalar1=math.sqrt(float(WIDTH)), scalar2=0.0, op0=ALU.mult, op1=ALU.add
+        )
+
+        def transposes(bank, src, first, k0):
+            for jj in range(2):
+                words = src[:, first + jj, k0 : k0 + 512].bitcast(F32)
+                for u in range(2):
+                    col = u * 256 + jj * P
+                    nc.tensor.transpose(bank[:, col : col + P], words[:, u * P : (u + 1) * P], identf[:])
+
+        def leave(on_vector, grp, half, bank):
+            dst = grp[:].bitcast(F32).rearrange("p (n u) -> p n u", u=2)[:, half * 256 : (half + 1) * 256, :]
+            src = bank[:].rearrange("p (u n) -> p n u", u=2)
+            if on_vector:
+                nc.vector.tensor_copy(out=dst, in_=src)
+            else:
+                nc.scalar.copy(out=dst, in_=src)
+
+        def quantise(grp, codes, scales):
+            nc.vector.quantize_mx(out=codes[:].bitcast(FP8X4), scales=scales[:], in_=grp[:])
+
+        def prepare_weight(raw, k0, name):
+            grp = wtmp.tile([P, 4 * GROUP], BF16, name="g" + name, tag="wgrp", align_bytes=64)
+            for half in range(2):
+                bank = pv.tile([P, 512], F32, name="b%s%d" % (name, half), tag="pv")
+                transposes(bank, raw, 2 * half, k0)
+                leave(True, grp, half, bank)
+            codes = const.tile([P, GROUP], U32, name="c" + name, align_bytes=64)
+            scales = const.tile([P, GROUP], U8, name="s" + name, align_bytes=64)
+            quantise(grp, codes, scales)
+            return codes, scales
+
+        bbank = pv.tile([P, 512], F32, name="bbank", tag="pv")
+        nc.tensor.transpose(bbank[:, 0:P], btile[:].bitcast(F32), identf[:])
+        bwords = const.tile([P, 8], F32, name="bwords")
+        nc.vector.tensor_copy(out=bwords[:, 0:6], in_=bbank[:, 0:6])
+        bias = const.tile([P, 12], F32, name="bias")
+        nc.vector.tensor_copy(out=bias[:], in_=bwords[:, 0:6].bitcast(BF16))
+        nbg = const.tile([P, 4], F32, name="nbg")
+        nc.vector.tensor_scalar(out=nbg[:], in0=bias[:, 8:12], scalar1=-1.0, scalar2=None, op0=ALU.mult)
+
+        OPS = (("rawc", "grpc", 2), ("rawx", "grpx", 3), ("rawq", "grpq", 2))
+
+        def ti(g, k):
+            st = groups[g]
+            raw_key, grp_key, bufs = OPS[k // 2]
+            half = k % 2
+            if half == 0:
+                st[grp_key] = grps.tile(
+                    [P, 4 * GROUP], BF16, name="%s%d" % (grp_key, g), tag=grp_key, bufs=bufs, align_bytes=64
+                )
+            bank = ps.tile([P, 512], F32, name="ti%d_%d" % (g, k), tag="ps")
+            transposes(bank, st[raw_key], 2 * half, 0)
+            leave(False, st[grp_key], half, bank)
+
+        def new_codes(g, key):
+            codes = cods.tile([P, GROUP], U32, name="c%s%d" % (key, g), tag="c" + key, align_bytes=64)
+            scales = cods.tile([P, GROUP], U8, name="s%s%d" % (key, g), tag="s" + key, align_bytes=64)
+            groups[g]["q" + key] = (codes, scales)
+            return codes, scales
+
+        def qz(g, key):
+            codes, scales = new_codes(g, key)
+            quantise(groups[g]["grp" + key], codes, scales)
+
+        weights = {}
+
+        def m1(g, j):
+            st = groups[g]
+            if j == 0:
+                st["grpr"] = work.tile([P, 4 * GROUP], BF16, name="grpr%d" % g, tag="grpr", align_bytes=64)
+            wc, ws = weights["w1"]
+            ac, asc = st["qc"]
+            bank = pv.tile([P, 512], F32, name="m1_%d_%d" % (g, j), tag="pv")
+            tok = slice(j * P, (j + 1) * P)
+            for c in range(4):
+                col = slice(c * P, (c + 1) * P)
+                nc.tensor.matmul_mx(
+                    out=bank[:, col],
+                    lhsT=wc[:, col].bitcast(FP8X4),
+                    lhsT_scale=ws[:, col],
+                    rhs=ac[:, tok].bitcast(FP8X4),
+                    rhs_scale=asc[:, tok],
+                    start=True,
+                    stop=True,
+                )
+            nc.vector.tensor_tensor(
+                out=st["grpr"][:].rearrange("p (n c) -> p n c", c=4)[:, tok, :],
+                in0=bank[:].rearrange("p (c n) -> p n c", c=4),
+                in1=bias[:, 0:4].unsqueeze(1).to_broadcast([P, P, 4]),
+                op=ALU.add,
+            )
+
+        def m3(g, c):
+            st = groups[g]
+            if c == 0:
+                st["h"] = work.tile([P, 4, GROUP], F32, name="h%d" % g, tag="h")
+            bank = ps.tile([P, 512], F32, name="m3_%d_%d" % (g, c), tag="ps")
+            col = slice(c * P, (c + 1) * P)
+            for n, (wkey, akey) in enumerate((("wgx", "qx"), ("wgq", "qq"))):
+                wc, ws = weights[wkey]
+                ac, asc = st[akey]
+                nc.tensor.matmul_mx(
+                    out=bank[:],
+                    lhsT=wc[:, col].bitcast(FP8X4),
+                    lhsT_scale=ws[:, col],
+                    rhs=ac[:].bitcast(FP8X4),
+                    rhs_scale=asc[:],
+                    start=(n == 0),
+                    stop=(n == 1),
+                )
+            nc.scalar.activation(
+                out=st["h"][:, c, :], in_=bank[:], func=ACT.Sigmoid, bias=nbg[:, c : c + 1], scale=-1.0
+            )
+
+        def m2(g, c):
+            st = groups[g]
+            if c == 0:
+                st["dy"] = work.tile([P, 4, GROUP], F32, name="dy%d" % g, tag="dy")
+            bank = pv.tile([P, 512], F32, name="m2_%d_%d" % (g, c), tag="pv")
+            col = slice(c * P, (c + 1) * P)
+            wc, ws = weights["w2"]
+            ac, asc = st["qr"]
+            nc.tensor.matmul_mx(
+                out=bank[:],
+                lhsT=wc[:, col].bitcast(FP8X4),
+                lhsT_scale=ws[:, col],
+                rhs=ac[:].bitcast(FP8X4),
+                rhs_scale=asc[:],
+                start=True,
+                stop=True,
+            )
+            nc.vector.scalar_tensor_tensor(
+                out=st["dy"][:, c, :],
+                in0=bank[:],
+                scalar=bias[:, 4 + c : 5 + c],
+                in1=st["grpx"][:].rearrange("p (n t) -> p n t", t=4)[:, :, c],
+                op0=ALU.add,
+                op1=ALU.subtract,
+            )
+
+        def cm(g, j):
+            st = groups[g]
+            tok = slice(j * P, (j + 1) * P)
+            nc.gpsimd.tensor_tensor(out=st["dy"][:, :, tok], in0=st["dy"][:, :, tok], in1=st["h"][:, :, tok], op=ALU.mult)
+
+        def tb(g, j):
+            st = groups[g]
+            if j == 0:
+                st["yc"] = work.tile([P, 4, WIDTH], F32, name="yc%d" % g, tag="yc")
+                for key in ("sums", "nmu", "ssq"):
+                    st[key] = stat.tile([P, 4], F32, name="%s%d" % (key, g), tag=key)
+            bank = ps.tile([P, 512], F32, name="tb%d_%d" % (g, j), tag="ps")
+            nc.tensor.matmul(
+                out=bank[:].rearrange("p (u e m) -> p u e m", u=2, e=2),
+                lhsT=identb[:],
+                rhs=st["rawx"][:, j, :].rearrange("p (u m e) -> p u e m", u=2, e=2),
+                start=True,
+                stop=False,
+            )
+            for c in range(4):
+                nc.tensor.matmul(
+                    out=bank[:, c * P : (c + 1) * P],
+                    lhsT=st["dy"][:, c, j * P : (j + 1) * P],
+                    rhs=identf[:],
+                    is_transpose=True,
+                    start=False,
+                    stop=(c == 3),
+                )
+            nc.scalar.activation(
+                out=st["yc"][:, j, :].rearrange("p (u m e) -> p u m e", u=2, e=2),
+                in_=bank[:].rearrange("p (u e m) -> p u m e", u=2, e=2),
+                func=ACT.Identity,
+                accum_out=st["sums"][:, j : j + 1],
+            )
+
+        def s2(g, j):
+            st = groups[g]
+            one = slice(j, j + 1)
+            nc.scalar.mul(out=st["nmu"][:, one], in_=st["sums"][:, one], mul=-1.0 / WIDTH)
+            nc.scalar.activation(
+                out=junk[:], in_=st["yc"][:, j, :], func=ACT.Square, bias=st["nmu"][:, one], scale=1.0,
+                accum_out=st["ssq"][:, one],
+            )
+
+        def pw(g, a):
+            st = groups[g]
+            if a == 0:
+                st["var"] = stat.tile([P, 4], F32, name="var%d" % g, tag="var")
+                st["rs"] = stat.tile([P, 4], F32, name="rs%d" % g, tag="rs")
+            two = slice(2 * a, 2 * a + 2)
+            nc.gpsimd.tensor_scalar(
+                out=st["var"][:, two], in0=st["ssq"][:, two], scalar1=WIDTH * LN_EPS, scalar2=1.0,
+                op0=ALU.add, op1=ALU.mult,
+            )
+            nc.gpsimd.tensor_tensor(out=st["rs"][:, two], in0=st["var"][:, two], in1=mhalf[:], op=ALU.pow)
+
+        def fg(g, j):
+            st = groups[g]
+            if j == 0:
+                st["o"] = work.tile([P, 4, WIDTH], F32, name="o%d" % g, tag="o")
+            one = slice(j, j + 1)
+            nc.vector.scalar_tensor_tensor(
+                out=st["o"][:, j, :], in0=st["yc"][:, j, :], scalar=st["nmu"][:, one], in1=lngs[:],
+                op0=ALU.add, op1=ALU.mult,
+            )
+            nc.vector.scalar_tensor_tensor(
+                out=st["o"][:, j, :], in0=st["o"][:, j, :], scalar=st["rs"][:, one], in1=lnb[:],
+                op0=ALU.mult, op1=ALU.add,
+            )
+            if j % 2 == 1:
+                rows = slice(g * GROUP, (g + 1) * GROUP)
+                nc.sync.dma_start(
+                    out=o_rows[rows, :].rearrange("(p j) d -> p j d", j=4)[:, j - 1 : j + 1, :],
+                    in_=st["o"][:, j - 1 : j + 1, :],
+                )
+
+        weights["w1"] = prepare_weight(w1raw, 0, "w1")
+        ti(0, 0)
+        ti(0, 1)
+        qz(0, "c")
+
+        for g in range(N_GROUPS):
+            nxt = g + 1 < N_GROUPS
+            prev = g > 0
+            if g + 2 < N_GROUPS:
+                load(g + 2)
+            for j in range(4):
+                m1(g, j)
+            qz(g, "r")
+            if g == 0:
+                for k in range(2, 6):
+                    ti(0, k)
+                qz(0, "x")
+                qz(0, "q")
+                weights["wgx"] = prepare_weight(wgraw, 0, "wgx")
+                weights["wgq"] = prepare_weight(wgraw, 512, "wgq")
+            for c in range(4):
+                m3(g, c)
+            if prev:
+                fg(g - 1, 0)
+            if g == 0:
+                weights["w2"] = prepare_weight(w2raw, 0, "w2")
+            for c in range(4):
+                m2(g, c)
+            if nxt:
+                for k in range(4):
+                    ti(g + 1, k)
+            if prev:
+                fg(g - 1, 1)
+            if nxt:
+                qz(g + 1, "c")
+            if prev:
+                fg(g - 1, 2)
+            if nxt:
+                qz(g + 1, "x")
+            cm(g, 0)
+            tb(g, 0)
+            if nxt:
+                ti(g + 1, 4)
+            s2(g, 0)
+            cm(g, 1)
+            tb(g, 1)
+            if nxt:
+                ti(g + 1, 5)
+            s2(g, 1)
+            if prev:
+                fg(g - 1, 3)
+            if nxt:
+                qz(g + 1, "q")
+            cm(g, 2)
+            tb(g, 2)
+            cm(g, 3)
+            tb(g, 3)
+            s2(g, 2)
+            s2(g, 3)
+            pw(g, 0)
+            pw(g, 1)
+        for j in range(4):
+            fg(N_GROUPS - 1, j)

@@ -15,7 +15,8 @@ ACT = mybir.ActivationFunctionType
 P = 128
 TOKENS = 4096
 WIDTH = 512
-GROUP = 512
+GROUP = 256
+SUPER = 512
 N_GROUPS = TOKENS // GROUP
 LN_EPS = 1e-5
 FLOPS = 2 * TOKENS * WIDTH * (512 + 512 + 1024)
@@ -38,12 +39,13 @@ def tile_rotelearningmemory_pa_t_kernel(
         const = stack.enter_context(tc.tile_pool(name="const", bufs=1))
         wtmp = stack.enter_context(tc.tile_pool(name="wtmp", bufs=2))
         raws = stack.enter_context(tc.tile_pool(name="raws", bufs=3))
-        grps = stack.enter_context(tc.tile_pool(name="grps", bufs=2))
-        cods = stack.enter_context(tc.tile_pool(name="cods", bufs=2))
-        work = stack.enter_context(tc.tile_pool(name="work", bufs=2))
-        stat = stack.enter_context(tc.tile_pool(name="stat", bufs=3))
+        grps = stack.enter_context(tc.tile_pool(name="grps", bufs=3))
+        cods = stack.enter_context(tc.tile_pool(name="cods", bufs=3))
+        work = stack.enter_context(tc.tile_pool(name="work", bufs=3))
+        stat = stack.enter_context(tc.tile_pool(name="stat", bufs=4))
+        pc = stack.enter_context(tc.psum_pool(name="pc", bufs=1))
         pv = stack.enter_context(tc.psum_pool(name="pv", bufs=3))
-        ps = stack.enter_context(tc.psum_pool(name="ps", bufs=5))
+        ps = stack.enter_context(tc.psum_pool(name="ps", bufs=4))
 
         identf = const.tile([P, P], F32, name="identf")
         make_identity(nc, identf[:])
@@ -66,14 +68,17 @@ def tile_rotelearningmemory_pa_t_kernel(
             )
             return raw
 
+        supers = {}
         groups = {}
+        for g in range(N_GROUPS):
+            groups[g] = {}
 
-        def load(g):
+        def load(s):
             st = {}
-            groups[g] = st
-            rows = slice(g * GROUP, (g + 1) * GROUP)
-            for key, src, bufs in (("rawc", c_rows, 3), ("rawx", x_rows, 4), ("rawq", q_rows, 3)):
-                raw = raws.tile([P, 4, WIDTH], BF16, name="%s%d" % (key, g), tag=key, bufs=bufs)
+            supers[s] = st
+            rows = slice(s * SUPER, (s + 1) * SUPER)
+            for key, src, bufs in (("c", c_rows, 3), ("x", x_rows, 4), ("q", q_rows, 3)):
+                raw = raws.tile([P, 4, WIDTH], BF16, name="raw%s%d" % (key, s), tag="raw" + key, bufs=bufs)
                 nc.sync.dma_start(out=raw[:], in_=src[rows, :].rearrange("(p j) k -> p j k", j=4))
                 st[key] = raw
 
@@ -81,16 +86,12 @@ def tile_rotelearningmemory_pa_t_kernel(
         load(0)
         wgraw = load_weight(gate_w, 1024, "wgraw")
         w2raw = load_weight(op_w, 512, "w2raw")
-        load(1)
 
         lng = const.tile([P, WIDTH], BF16, name="lng")
         nc.scalar.dma_start(out=lng[:], in_=ln_g.partition_broadcast(P))
         lnb = const.tile([P, WIDTH], BF16, name="lnb")
         nc.scalar.dma_start(out=lnb[:], in_=ln_b.partition_broadcast(P))
-        lngs = const.tile([P, WIDTH], F32, name="lngs")
-        nc.gpsimd.tensor_scalar(
-            out=lngs[:], in0=lng[:], scalar1=math.sqrt(float(WIDTH)), scalar2=0.0, op0=ALU.mult, op1=ALU.add
-        )
+        lnbank = pc.tile([P, 2 * WIDTH], BF16, name="lnbank")
 
         def transposes(bank, src, first, k0):
             for jj in range(2):
@@ -99,26 +100,25 @@ def tile_rotelearningmemory_pa_t_kernel(
                     col = u * 256 + jj * P
                     nc.tensor.transpose(bank[:, col : col + P], words[:, u * P : (u + 1) * P], identf[:])
 
-        def leave(on_vector, grp, half, bank):
-            dst = grp[:].bitcast(F32).rearrange("p (n u) -> p n u", u=2)[:, half * 256 : (half + 1) * 256, :]
+        def leave(on_vector, dst, bank):
             src = bank[:].rearrange("p (u n) -> p n u", u=2)
             if on_vector:
                 nc.vector.tensor_copy(out=dst, in_=src)
             else:
                 nc.scalar.copy(out=dst, in_=src)
 
-        def quantise(grp, codes, scales):
-            nc.vector.quantize_mx(out=codes[:].bitcast(FP8X4), scales=scales[:], in_=grp[:])
+        def words_of(grp):
+            return grp[:].bitcast(F32).rearrange("p (n u) -> p n u", u=2)
 
         def prepare_weight(raw, k0, name):
-            grp = wtmp.tile([P, 4 * GROUP], BF16, name="g" + name, tag="wgrp", align_bytes=64)
+            grp = wtmp.tile([P, 2048], BF16, name="g" + name, tag="wgrp", align_bytes=64)
             for half in range(2):
                 bank = pv.tile([P, 512], F32, name="b%s%d" % (name, half), tag="pv")
                 transposes(bank, raw, 2 * half, k0)
-                leave(True, grp, half, bank)
-            codes = const.tile([P, GROUP], U32, name="c" + name, align_bytes=64)
-            scales = const.tile([P, GROUP], U8, name="s" + name, align_bytes=64)
-            quantise(grp, codes, scales)
+                leave(True, words_of(grp)[:, half * 256 : (half + 1) * 256, :], bank)
+            codes = const.tile([P, 512], U32, name="c" + name, align_bytes=64)
+            scales = const.tile([P, 512], U8, name="s" + name, align_bytes=64)
+            nc.vector.quantize_mx(out=codes[:].bitcast(FP8X4), scales=scales[:], in_=grp[:])
             return codes, scales
 
         bbank = pv.tile([P, 512], F32, name="bbank", tag="pv")
@@ -130,51 +130,55 @@ def tile_rotelearningmemory_pa_t_kernel(
         nbg = const.tile([P, 4], F32, name="nbg")
         nc.vector.tensor_scalar(out=nbg[:], in0=bias[:, 8:12], scalar1=-1.0, scalar2=None, op0=ALU.mult)
 
-        OPS = (("rawc", "grpc", 2), ("rawx", "grpx", 3), ("rawq", "grpq", 2))
+        weights = {}
+        GRP_BUFS = {"c": 3, "x": 4, "q": 3}
 
-        def ti(g, k):
+        def ok(g):
+            return 0 <= g < N_GROUPS
+
+        def ti(g, key):
+            if not ok(g):
+                return
             st = groups[g]
-            raw_key, grp_key, bufs = OPS[k // 2]
-            half = k % 2
-            if half == 0:
-                st[grp_key] = grps.tile(
-                    [P, 4 * GROUP], BF16, name="%s%d" % (grp_key, g), tag=grp_key, bufs=bufs, align_bytes=64
-                )
-            bank = ps.tile([P, 512], F32, name="ti%d_%d" % (g, k), tag="ps")
-            transposes(bank, st[raw_key], 2 * half, 0)
-            leave(False, st[grp_key], half, bank)
-
-        def new_codes(g, key):
-            codes = cods.tile([P, GROUP], U32, name="c%s%d" % (key, g), tag="c" + key, align_bytes=64)
-            scales = cods.tile([P, GROUP], U8, name="s%s%d" % (key, g), tag="s" + key, align_bytes=64)
-            groups[g]["q" + key] = (codes, scales)
-            return codes, scales
+            grp = grps.tile([P, 4 * GROUP], BF16, name="grp%s%d" % (key, g), tag="grp" + key, bufs=GRP_BUFS[key], align_bytes=64)
+            st["grp" + key] = grp
+            bank = ps.tile([P, 512], F32, name="ti%s%d" % (key, g), tag="ps")
+            transposes(bank, supers[g // 2][key], 2 * (g % 2), 0)
+            leave(False, words_of(grp), bank)
 
         def qz(g, key):
-            codes, scales = new_codes(g, key)
-            quantise(groups[g]["grp" + key], codes, scales)
-
-        weights = {}
-
-        def m1(g, j):
+            if not ok(g):
+                return
             st = groups[g]
-            if j == 0:
+            codes = cods.tile([P, GROUP], U32, name="c%s%d" % (key, g), tag="c" + key, align_bytes=64)
+            scales = cods.tile([P, GROUP], U8, name="s%s%d" % (key, g), tag="s" + key, align_bytes=64)
+            st["q" + key] = (codes, scales)
+            nc.vector.quantize_mx(out=codes[:].bitcast(FP8X4), scales=scales[:], in_=st["grp" + key][:])
+
+        def mx(out, wkey, c, act, cols, start, stop):
+            wc, ws = weights[wkey]
+            ac, asc = act
+            col = slice(c * P, (c + 1) * P)
+            nc.tensor.matmul_mx(
+                out=out,
+                lhsT=wc[:, col].bitcast(FP8X4),
+                lhsT_scale=ws[:, col],
+                rhs=ac[:, cols].bitcast(FP8X4),
+                rhs_scale=asc[:, cols],
+                start=start,
+                stop=stop,
+            )
+
+        def m1(g, jj):
+            if not ok(g):
+                return
+            st = groups[g]
+            if jj == 0:
                 st["grpr"] = work.tile([P, 4 * GROUP], BF16, name="grpr%d" % g, tag="grpr", align_bytes=64)
-            wc, ws = weights["w1"]
-            ac, asc = st["qc"]
-            bank = pv.tile([P, 512], F32, name="m1_%d_%d" % (g, j), tag="pv")
-            tok = slice(j * P, (j + 1) * P)
+            bank = pv.tile([P, 512], F32, name="m1_%d_%d" % (g, jj), tag="pv")
+            tok = slice(jj * P, (jj + 1) * P)
             for c in range(4):
-                col = slice(c * P, (c + 1) * P)
-                nc.tensor.matmul_mx(
-                    out=bank[:, col],
-                    lhsT=wc[:, col].bitcast(FP8X4),
-                    lhsT_scale=ws[:, col],
-                    rhs=ac[:, tok].bitcast(FP8X4),
-                    rhs_scale=asc[:, tok],
-                    start=True,
-                    stop=True,
-                )
+                mx(bank[:, c * P : (c + 1) * P], "w1", c, st["qc"], tok, True, True)
             nc.vector.tensor_tensor(
                 out=st["grpr"][:].rearrange("p (n c) -> p n c", c=4)[:, tok, :],
                 in0=bank[:].rearrange("p (c n) -> p n c", c=4),
@@ -182,190 +186,161 @@ def tile_rotelearningmemory_pa_t_kernel(
                 op=ALU.add,
             )
 
-        def m3(g, c):
+        def m3(g, b):
+            if not ok(g):
+                return
             st = groups[g]
-            if c == 0:
+            if b == 0:
                 st["h"] = work.tile([P, 4, GROUP], F32, name="h%d" % g, tag="h")
-            bank = ps.tile([P, 512], F32, name="m3_%d_%d" % (g, c), tag="ps")
-            col = slice(c * P, (c + 1) * P)
-            for n, (wkey, akey) in enumerate((("wgx", "qx"), ("wgq", "qq"))):
-                wc, ws = weights[wkey]
-                ac, asc = st[akey]
-                nc.tensor.matmul_mx(
-                    out=bank[:],
-                    lhsT=wc[:, col].bitcast(FP8X4),
-                    lhsT_scale=ws[:, col],
-                    rhs=ac[:].bitcast(FP8X4),
-                    rhs_scale=asc[:],
-                    start=(n == 0),
-                    stop=(n == 1),
+            bank = ps.tile([P, 512], F32, name="m3_%d_%d" % (g, b), tag="ps")
+            every = slice(0, GROUP)
+            for cc in range(2):
+                part = bank[:, cc * GROUP : (cc + 1) * GROUP]
+                mx(part, "wgx", 2 * b + cc, st["qx"], every, True, False)
+                mx(part, "wgq", 2 * b + cc, st["qq"], every, False, True)
+            for cc in range(2):
+                c = 2 * b + cc
+                nc.scalar.activation(
+                    out=st["h"][:, c, :], in_=bank[:, cc * GROUP : (cc + 1) * GROUP], func=ACT.Sigmoid,
+                    bias=nbg[:, c : c + 1], scale=-1.0,
                 )
-            nc.scalar.activation(
-                out=st["h"][:, c, :], in_=bank[:], func=ACT.Sigmoid, bias=nbg[:, c : c + 1], scale=-1.0
-            )
 
-        def m2(g, c):
+        def m2(g, b):
+            if not ok(g):
+                return
             st = groups[g]
-            if c == 0:
+            if b == 0:
                 st["dy"] = work.tile([P, 4, GROUP], F32, name="dy%d" % g, tag="dy")
-            bank = pv.tile([P, 512], F32, name="m2_%d_%d" % (g, c), tag="pv")
-            col = slice(c * P, (c + 1) * P)
-            wc, ws = weights["w2"]
-            ac, asc = st["qr"]
-            nc.tensor.matmul_mx(
-                out=bank[:],
-                lhsT=wc[:, col].bitcast(FP8X4),
-                lhsT_scale=ws[:, col],
-                rhs=ac[:].bitcast(FP8X4),
-                rhs_scale=asc[:],
-                start=True,
-                stop=True,
-            )
-            nc.vector.scalar_tensor_tensor(
-                out=st["dy"][:, c, :],
-                in0=bank[:],
-                scalar=bias[:, 4 + c : 5 + c],
-                in1=st["grpx"][:].rearrange("p (n t) -> p n t", t=4)[:, :, c],
-                op0=ALU.add,
-                op1=ALU.subtract,
-            )
+            bank = pv.tile([P, 512], F32, name="m2_%d_%d" % (g, b), tag="pv")
+            for cc in range(2):
+                mx(bank[:, cc * GROUP : (cc + 1) * GROUP], "w2", 2 * b + cc, st["qr"], slice(0, GROUP), True, True)
+            for cc in range(2):
+                c = 2 * b + cc
+                nc.vector.scalar_tensor_tensor(
+                    out=st["dy"][:, c, :],
+                    in0=bank[:, cc * GROUP : (cc + 1) * GROUP],
+                    scalar=bias[:, 4 + c : 5 + c],
+                    in1=st["grpx"][:].rearrange("p (n t) -> p n t", t=4)[:, :, c],
+                    op0=ALU.add,
+                    op1=ALU.subtract,
+                )
 
-        def cm(g, j):
+        def cm(g, jj):
+            if not ok(g):
+                return
             st = groups[g]
-            tok = slice(j * P, (j + 1) * P)
+            tok = slice(jj * P, (jj + 1) * P)
             nc.gpsimd.tensor_tensor(out=st["dy"][:, :, tok], in0=st["dy"][:, :, tok], in1=st["h"][:, :, tok], op=ALU.mult)
 
-        def tb(g, j):
+        def tb(g, jj):
+            if not ok(g):
+                return
             st = groups[g]
-            if j == 0:
-                st["yc"] = work.tile([P, 4, WIDTH], F32, name="yc%d" % g, tag="yc")
+            if jj == 0:
+                st["yc"] = work.tile([P, 2, WIDTH], F32, name="yc%d" % g, tag="yc")
                 for key in ("sums", "nmu", "ssq"):
-                    st[key] = stat.tile([P, 4], F32, name="%s%d" % (key, g), tag=key)
-            bank = ps.tile([P, 512], F32, name="tb%d_%d" % (g, j), tag="ps")
+                    st[key] = stat.tile([P, 2], F32, name="%s%d" % (key, g), tag=key)
+            bank = ps.tile([P, 512], F32, name="tb%d_%d" % (g, jj), tag="ps")
             nc.tensor.matmul(
                 out=bank[:].rearrange("p (u e m) -> p u e m", u=2, e=2),
                 lhsT=identb[:],
-                rhs=st["rawx"][:, j, :].rearrange("p (u m e) -> p u e m", u=2, e=2),
+                rhs=supers[g // 2]["x"][:, 2 * (g % 2) + jj, :].rearrange("p (u m e) -> p u e m", u=2, e=2),
                 start=True,
                 stop=False,
             )
             for c in range(4):
                 nc.tensor.matmul(
                     out=bank[:, c * P : (c + 1) * P],
-                    lhsT=st["dy"][:, c, j * P : (j + 1) * P],
+                    lhsT=st["dy"][:, c, jj * P : (jj + 1) * P],
                     rhs=identf[:],
                     is_transpose=True,
                     start=False,
                     stop=(c == 3),
                 )
             nc.scalar.activation(
-                out=st["yc"][:, j, :].rearrange("p (u m e) -> p u m e", u=2, e=2),
+                out=st["yc"][:, jj, :].rearrange("p (u m e) -> p u m e", u=2, e=2),
                 in_=bank[:].rearrange("p (u e m) -> p u m e", u=2, e=2),
                 func=ACT.Identity,
-                accum_out=st["sums"][:, j : j + 1],
+                accum_out=st["sums"][:, jj : jj + 1],
             )
 
-        def s2(g, j):
+        def s2(g, jj):
+            if not ok(g):
+                return
             st = groups[g]
-            one = slice(j, j + 1)
+            one = slice(jj, jj + 1)
             nc.scalar.mul(out=st["nmu"][:, one], in_=st["sums"][:, one], mul=-1.0 / WIDTH)
             nc.scalar.activation(
-                out=junk[:], in_=st["yc"][:, j, :], func=ACT.Square, bias=st["nmu"][:, one], scale=1.0,
+                out=junk[:], in_=st["yc"][:, jj, :], func=ACT.Square, bias=st["nmu"][:, one], scale=1.0,
                 accum_out=st["ssq"][:, one],
             )
 
-        def pw(g, a):
+        def pw(g):
+            if not ok(g):
+                return
             st = groups[g]
-            if a == 0:
-                st["var"] = stat.tile([P, 4], F32, name="var%d" % g, tag="var")
-                st["rs"] = stat.tile([P, 4], F32, name="rs%d" % g, tag="rs")
-            two = slice(2 * a, 2 * a + 2)
+            st["var"] = stat.tile([P, 2], F32, name="var%d" % g, tag="var")
+            st["rs"] = stat.tile([P, 2], F32, name="rs%d" % g, tag="rs")
             nc.gpsimd.tensor_scalar(
-                out=st["var"][:, two], in0=st["ssq"][:, two], scalar1=WIDTH * LN_EPS, scalar2=1.0,
-                op0=ALU.add, op1=ALU.mult,
+                out=st["var"][:], in0=st["ssq"][:], scalar1=1.0 / WIDTH, scalar2=LN_EPS, op0=ALU.mult, op1=ALU.add
             )
-            nc.gpsimd.tensor_tensor(out=st["rs"][:, two], in0=st["var"][:, two], in1=mhalf[:], op=ALU.pow)
+            nc.gpsimd.tensor_tensor(out=st["rs"][:], in0=st["var"][:], in1=mhalf[:], op=ALU.pow)
 
-        def fg(g, j):
+        def fg(g, jj):
+            if not ok(g):
+                return
             st = groups[g]
-            if j == 0:
-                st["o"] = work.tile([P, 4, WIDTH], F32, name="o%d" % g, tag="o")
-            one = slice(j, j + 1)
+            if jj == 0:
+                st["o"] = work.tile([P, 2, WIDTH], F32, name="o%d" % g, tag="o")
+            one = slice(jj, jj + 1)
             nc.vector.scalar_tensor_tensor(
-                out=st["o"][:, j, :], in0=st["yc"][:, j, :], scalar=st["nmu"][:, one], in1=lngs[:],
+                out=st["o"][:, jj, :], in0=st["yc"][:, jj, :], scalar=st["nmu"][:, one], in1=lnbank[:, 0:WIDTH],
                 op0=ALU.add, op1=ALU.mult,
             )
             nc.vector.scalar_tensor_tensor(
-                out=st["o"][:, j, :], in0=st["o"][:, j, :], scalar=st["rs"][:, one], in1=lnb[:],
+                out=st["o"][:, jj, :], in0=st["o"][:, jj, :], scalar=st["rs"][:, one], in1=lnbank[:, WIDTH : 2 * WIDTH],
                 op0=ALU.mult, op1=ALU.add,
             )
-            if j % 2 == 1:
-                rows = slice(g * GROUP, (g + 1) * GROUP)
+            if jj == 1:
+                s = g // 2
+                first = 2 * (g % 2)
                 nc.sync.dma_start(
-                    out=o_rows[rows, :].rearrange("(p j) d -> p j d", j=4)[:, j - 1 : j + 1, :],
-                    in_=st["o"][:, j - 1 : j + 1, :],
+                    out=o_rows[s * SUPER : (s + 1) * SUPER, :].rearrange("(p j) d -> p j d", j=4)[:, first : first + 2, :],
+                    in_=st["o"][:],
                 )
 
-        weights["w1"] = prepare_weight(w1raw, 0, "w1")
-        ti(0, 0)
-        ti(0, 1)
-        qz(0, "c")
-
-        for g in range(N_GROUPS):
-            nxt = g + 1 < N_GROUPS
-            prev = g > 0
-            if g + 2 < N_GROUPS:
-                load(g + 2)
-            for j in range(4):
-                m1(g, j)
-            qz(g, "r")
-            if g == 0:
-                for k in range(2, 6):
-                    ti(0, k)
-                qz(0, "x")
-                qz(0, "q")
+        for t in range(-2, N_GROUPS + 3):
+            if t % 2 == 0 and 0 < (t + 4) // 2 < N_GROUPS // 2:
+                load((t + 4) // 2)
+            qz(t + 1, "c")
+            m1(t, 0)
+            m1(t, 1)
+            qz(t, "r")
+            pw(t - 3)
+            cm(t - 1, 0)
+            cm(t - 1, 1)
+            if t == -2:
+                weights["w1"] = prepare_weight(w1raw, 0, "w1")
+            if t == -1:
                 weights["wgx"] = prepare_weight(wgraw, 0, "wgx")
                 weights["wgq"] = prepare_weight(wgraw, 512, "wgq")
-            for c in range(4):
-                m3(g, c)
-            if prev:
-                fg(g - 1, 0)
-            if g == 0:
+            if t == 0:
                 weights["w2"] = prepare_weight(w2raw, 0, "w2")
-            for c in range(4):
-                m2(g, c)
-            if nxt:
-                for k in range(4):
-                    ti(g + 1, k)
-            if prev:
-                fg(g - 1, 1)
-            if nxt:
-                qz(g + 1, "c")
-            if prev:
-                fg(g - 1, 2)
-            if nxt:
-                qz(g + 1, "x")
-            cm(g, 0)
-            tb(g, 0)
-            if nxt:
-                ti(g + 1, 4)
-            s2(g, 0)
-            cm(g, 1)
-            tb(g, 1)
-            if nxt:
-                ti(g + 1, 5)
-            s2(g, 1)
-            if prev:
-                fg(g - 1, 3)
-            if nxt:
-                qz(g + 1, "q")
-            cm(g, 2)
-            tb(g, 2)
-            cm(g, 3)
-            tb(g, 3)
-            s2(g, 2)
-            s2(g, 3)
-            pw(g, 0)
-            pw(g, 1)
-        for j in range(4):
-            fg(N_GROUPS - 1, j)
+            if t == 1:
+                nc.tensor.matmul(out=lnbank[:, 0:WIDTH], lhsT=identb[:], rhs=lng[:], start=True, stop=True)
+                nc.tensor.matmul(out=lnbank[:, WIDTH : 2 * WIDTH], lhsT=identb[:], rhs=lnb[:], start=True, stop=True)
+            ti(t + 2, "c")
+            tb(t - 2, 0)
+            fg(t - 3, 0)
+            qz(t + 1, "x")
+            m3(t, 0)
+            s2(t - 2, 0)
+            m3(t, 1)
+            m2(t, 0)
+            m2(t, 1)
+            ti(t + 2, "x")
+            tb(t - 2, 1)
+            ti(t + 2, "q")
+            s2(t - 2, 1)
+            fg(t - 3, 1)
+            qz(t + 1, "q")

@@ -39,7 +39,7 @@ def tile_rotelearningmemory_pa_t_kernel(
         const = stack.enter_context(tc.tile_pool(name="const", bufs=1))
         wtmp = stack.enter_context(tc.tile_pool(name="wtmp", bufs=2))
         raws = stack.enter_context(tc.tile_pool(name="raws", bufs=3))
-        grps = stack.enter_context(tc.tile_pool(name="grps", bufs=3))
+        grps = stack.enter_context(tc.tile_pool(name="grps", bufs=4))
         cods = stack.enter_context(tc.tile_pool(name="cods", bufs=3))
         work = stack.enter_context(tc.tile_pool(name="work", bufs=3))
         stat = stack.enter_context(tc.tile_pool(name="stat", bufs=4))
@@ -131,40 +131,60 @@ def tile_rotelearningmemory_pa_t_kernel(
         nc.vector.tensor_scalar(out=nbg[:], in0=bias[:, 8:12], scalar1=-1.0, scalar2=None, op0=ALU.mult)
 
         weights = {}
-        GRP_BUFS = {"c": 3, "x": 4, "q": 3}
+        SECTION = {"r": 0, "c": 1, "x": 2, "q": 3}
+        steps = {}
 
         def ok(g):
             return 0 <= g < N_GROUPS
 
+        def step_of(g, key):
+            return g if key == "r" else g - 1
+
+        def grouped(g, key):
+            t = step_of(g, key)
+            if t not in steps:
+                steps[t] = {"grp": grps.tile([P, 16 * GROUP], BF16, name="grp%d" % (t + 1), tag="grp", align_bytes=64)}
+            first = SECTION[key] * 4 * GROUP
+            return steps[t]["grp"][:, first : first + 4 * GROUP]
+
+        def quantise_step(t):
+            if t < -1 or t >= N_GROUPS:
+                return
+            st = steps[t]
+            st["codes"] = cods.tile([P, 4 * GROUP], U32, name="codes%d" % (t + 1), tag="codes", align_bytes=64)
+            st["scales"] = cods.tile([P, 4 * GROUP], U8, name="scales%d" % (t + 1), tag="scales", align_bytes=64)
+            if t == -1:
+                spans = ((1, 2), (2, 4))
+            elif t == N_GROUPS - 1:
+                spans = ((0, 1),)
+            else:
+                spans = ((0, 4),)
+            for a, b in spans:
+                nc.vector.quantize_mx(
+                    out=st["codes"][:, a * GROUP : b * GROUP].bitcast(FP8X4),
+                    scales=st["scales"][:, a * GROUP : b * GROUP],
+                    in_=st["grp"][:, 4 * a * GROUP : 4 * b * GROUP],
+                )
+
         def ti(g, key):
             if not ok(g):
                 return
-            st = groups[g]
-            grp = grps.tile([P, 4 * GROUP], BF16, name="grp%s%d" % (key, g), tag="grp" + key, bufs=GRP_BUFS[key], align_bytes=64)
-            st["grp" + key] = grp
+            grp = grouped(g, key)
             bank = ps.tile([P, 512], F32, name="ti%s%d" % (key, g), tag="ps")
             transposes(bank, supers[g // 2][key], 2 * (g % 2), 0)
-            leave(False, words_of(grp), bank)
+            leave(False, grp.bitcast(F32).rearrange("p (n u) -> p n u", u=2), bank)
 
-        def qz(g, key):
-            if not ok(g):
-                return
-            st = groups[g]
-            codes = cods.tile([P, GROUP], U32, name="c%s%d" % (key, g), tag="c" + key, align_bytes=64)
-            scales = cods.tile([P, GROUP], U8, name="s%s%d" % (key, g), tag="s" + key, align_bytes=64)
-            st["q" + key] = (codes, scales)
-            nc.vector.quantize_mx(out=codes[:].bitcast(FP8X4), scales=scales[:], in_=st["grp" + key][:])
-
-        def mx(out, wkey, c, act, cols, start, stop):
+        def mx(out, wkey, c, g, key, first, count, start, stop):
             wc, ws = weights[wkey]
-            ac, asc = act
+            st = steps[step_of(g, key)]
             col = slice(c * P, (c + 1) * P)
+            cols = slice(SECTION[key] * GROUP + first, SECTION[key] * GROUP + first + count)
             nc.tensor.matmul_mx(
                 out=out,
                 lhsT=wc[:, col].bitcast(FP8X4),
                 lhsT_scale=ws[:, col],
-                rhs=ac[:, cols].bitcast(FP8X4),
-                rhs_scale=asc[:, cols],
+                rhs=st["codes"][:, cols].bitcast(FP8X4),
+                rhs_scale=st["scales"][:, cols],
                 start=start,
                 stop=stop,
             )
@@ -172,15 +192,11 @@ def tile_rotelearningmemory_pa_t_kernel(
         def m1(g, jj):
             if not ok(g):
                 return
-            st = groups[g]
-            if jj == 0:
-                st["grpr"] = work.tile([P, 4 * GROUP], BF16, name="grpr%d" % g, tag="grpr", align_bytes=64)
             bank = pv.tile([P, 512], F32, name="m1_%d_%d" % (g, jj), tag="pv")
-            tok = slice(jj * P, (jj + 1) * P)
             for c in range(4):
-                mx(bank[:, c * P : (c + 1) * P], "w1", c, st["qc"], tok, True, True)
+                mx(bank[:, c * P : (c + 1) * P], "w1", c, g, "c", jj * P, P, True, True)
             nc.vector.tensor_tensor(
-                out=st["grpr"][:].rearrange("p (n c) -> p n c", c=4)[:, tok, :],
+                out=grouped(g, "r").rearrange("p (n c) -> p n c", c=4)[:, jj * P : (jj + 1) * P, :],
                 in0=bank[:].rearrange("p (c n) -> p n c", c=4),
                 in1=bias[:, 0:4].unsqueeze(1).to_broadcast([P, P, 4]),
                 op=ALU.add,
@@ -193,11 +209,10 @@ def tile_rotelearningmemory_pa_t_kernel(
             if b == 0:
                 st["h"] = work.tile([P, 4, GROUP], F32, name="h%d" % g, tag="h")
             bank = ps.tile([P, 512], F32, name="m3_%d_%d" % (g, b), tag="ps")
-            every = slice(0, GROUP)
             for cc in range(2):
                 part = bank[:, cc * GROUP : (cc + 1) * GROUP]
-                mx(part, "wgx", 2 * b + cc, st["qx"], every, True, False)
-                mx(part, "wgq", 2 * b + cc, st["qq"], every, False, True)
+                mx(part, "wgx", 2 * b + cc, g, "x", 0, GROUP, True, False)
+                mx(part, "wgq", 2 * b + cc, g, "q", 0, GROUP, False, True)
             for cc in range(2):
                 c = 2 * b + cc
                 nc.scalar.activation(
@@ -213,14 +228,14 @@ def tile_rotelearningmemory_pa_t_kernel(
                 st["dy"] = work.tile([P, 4, GROUP], F32, name="dy%d" % g, tag="dy")
             bank = pv.tile([P, 512], F32, name="m2_%d_%d" % (g, b), tag="pv")
             for cc in range(2):
-                mx(bank[:, cc * GROUP : (cc + 1) * GROUP], "w2", 2 * b + cc, st["qr"], slice(0, GROUP), True, True)
+                mx(bank[:, cc * GROUP : (cc + 1) * GROUP], "w2", 2 * b + cc, g, "r", 0, GROUP, True, True)
             for cc in range(2):
                 c = 2 * b + cc
                 nc.vector.scalar_tensor_tensor(
                     out=st["dy"][:, c, :],
                     in0=bank[:, cc * GROUP : (cc + 1) * GROUP],
                     scalar=bias[:, 4 + c : 5 + c],
-                    in1=st["grpx"][:].rearrange("p (n t) -> p n t", t=4)[:, :, c],
+                    in1=grouped(g, "x").rearrange("p (n t) -> p n t", t=4)[:, :, c],
                     op0=ALU.add,
                     op1=ALU.subtract,
                 )
@@ -264,12 +279,17 @@ def tile_rotelearningmemory_pa_t_kernel(
                 accum_out=st["sums"][:, jj : jj + 1],
             )
 
+        def mean(g):
+            if not ok(g):
+                return
+            st = groups[g]
+            nc.scalar.mul(out=st["nmu"][:], in_=st["sums"][:], mul=-1.0 / WIDTH)
+
         def s2(g, jj):
             if not ok(g):
                 return
             st = groups[g]
             one = slice(jj, jj + 1)
-            nc.scalar.mul(out=st["nmu"][:, one], in_=st["sums"][:, one], mul=-1.0 / WIDTH)
             nc.scalar.activation(
                 out=junk[:], in_=st["yc"][:, jj, :], func=ACT.Square, bias=st["nmu"][:, one], scale=1.0,
                 accum_out=st["ssq"][:, one],
@@ -286,20 +306,24 @@ def tile_rotelearningmemory_pa_t_kernel(
             )
             nc.gpsimd.tensor_tensor(out=st["rs"][:], in0=st["var"][:], in1=mhalf[:], op=ALU.pow)
 
-        def fg(g, jj):
+        def ln1(g, jj):
             if not ok(g):
                 return
             st = groups[g]
             if jj == 0:
                 st["o"] = work.tile([P, 2, WIDTH], F32, name="o%d" % g, tag="o")
-            one = slice(jj, jj + 1)
             nc.vector.scalar_tensor_tensor(
-                out=st["o"][:, jj, :], in0=st["yc"][:, jj, :], scalar=st["nmu"][:, one], in1=lnbank[:, 0:WIDTH],
+                out=st["o"][:, jj, :], in0=st["yc"][:, jj, :], scalar=st["nmu"][:, jj : jj + 1], in1=lnbank[:, 0:WIDTH],
                 op0=ALU.add, op1=ALU.mult,
             )
+
+        def ln2(g, jj):
+            if not ok(g):
+                return
+            st = groups[g]
             nc.vector.scalar_tensor_tensor(
-                out=st["o"][:, jj, :], in0=st["o"][:, jj, :], scalar=st["rs"][:, one], in1=lnbank[:, WIDTH : 2 * WIDTH],
-                op0=ALU.mult, op1=ALU.add,
+                out=st["o"][:, jj, :], in0=st["o"][:, jj, :], scalar=st["rs"][:, jj : jj + 1],
+                in1=lnbank[:, WIDTH : 2 * WIDTH], op0=ALU.mult, op1=ALU.add,
             )
             if jj == 1:
                 s = g // 2
@@ -312,13 +336,16 @@ def tile_rotelearningmemory_pa_t_kernel(
         for t in range(-2, N_GROUPS + 3):
             if t % 2 == 0 and 0 < (t + 4) // 2 < N_GROUPS // 2:
                 load((t + 4) // 2)
-            qz(t + 1, "c")
+            s2(t - 3, 0)
+            s2(t - 3, 1)
             m1(t, 0)
             m1(t, 1)
-            qz(t, "r")
-            pw(t - 3)
             cm(t - 1, 0)
             cm(t - 1, 1)
+            pw(t - 3)
+            ln1(t - 3, 0)
+            quantise_step(t)
+            ln1(t - 3, 1)
             if t == -2:
                 weights["w1"] = prepare_weight(w1raw, 0, "w1")
             if t == -1:
@@ -331,16 +358,13 @@ def tile_rotelearningmemory_pa_t_kernel(
                 nc.tensor.matmul(out=lnbank[:, WIDTH : 2 * WIDTH], lhsT=identb[:], rhs=lnb[:], start=True, stop=True)
             ti(t + 2, "c")
             tb(t - 2, 0)
-            fg(t - 3, 0)
-            qz(t + 1, "x")
+            ti(t + 2, "x")
+            ln2(t - 3, 0)
+            ln2(t - 3, 1)
             m3(t, 0)
-            s2(t - 2, 0)
             m3(t, 1)
             m2(t, 0)
             m2(t, 1)
-            ti(t + 2, "x")
             tb(t - 2, 1)
             ti(t + 2, "q")
-            s2(t - 2, 1)
-            fg(t - 3, 1)
-            qz(t + 1, "q")
+            mean(t - 2)

@@ -39,13 +39,12 @@ def tile_rotelearningmemory_pa_t_kernel(
         const = stack.enter_context(tc.tile_pool(name="const", bufs=1))
         wtmp = stack.enter_context(tc.tile_pool(name="wtmp", bufs=2))
         raws = stack.enter_context(tc.tile_pool(name="raws", bufs=3))
-        grps = stack.enter_context(tc.tile_pool(name="grps", bufs=4))
+        grps = stack.enter_context(tc.tile_pool(name="grps", bufs=3))
         cods = stack.enter_context(tc.tile_pool(name="cods", bufs=3))
         work = stack.enter_context(tc.tile_pool(name="work", bufs=3))
         stat = stack.enter_context(tc.tile_pool(name="stat", bufs=4))
         pc = stack.enter_context(tc.psum_pool(name="pc", bufs=1))
-        pv = stack.enter_context(tc.psum_pool(name="pv", bufs=3))
-        ps = stack.enter_context(tc.psum_pool(name="ps", bufs=4))
+        banks = stack.enter_context(tc.psum_pool(name="banks", bufs=7))
 
         identf = const.tile([P, P], F32, name="identf")
         make_identity(nc, identf[:])
@@ -77,7 +76,7 @@ def tile_rotelearningmemory_pa_t_kernel(
             st = {}
             supers[s] = st
             rows = slice(s * SUPER, (s + 1) * SUPER)
-            for key, src, bufs in (("c", c_rows, 3), ("x", x_rows, 4), ("q", q_rows, 3)):
+            for key, src, bufs in (("c", c_rows, 3), ("x", x_rows, 6), ("q", q_rows, 3)):
                 raw = raws.tile([P, 4, WIDTH], BF16, name="raw%s%d" % (key, s), tag="raw" + key, bufs=bufs)
                 nc.sync.dma_start(out=raw[:], in_=src[rows, :].rearrange("(p j) k -> p j k", j=4))
                 st[key] = raw
@@ -113,7 +112,7 @@ def tile_rotelearningmemory_pa_t_kernel(
         def prepare_weight(raw, k0, name):
             grp = wtmp.tile([P, 2048], BF16, name="g" + name, tag="wgrp", align_bytes=64)
             for half in range(2):
-                bank = pv.tile([P, 512], F32, name="b%s%d" % (name, half), tag="pv")
+                bank = banks.tile([P, 512], F32, name="b%s%d" % (name, half), tag="bank")
                 transposes(bank, raw, 2 * half, k0)
                 leave(True, words_of(grp)[:, half * 256 : (half + 1) * 256, :], bank)
             codes = const.tile([P, 512], U32, name="c" + name, align_bytes=64)
@@ -121,7 +120,7 @@ def tile_rotelearningmemory_pa_t_kernel(
             nc.vector.quantize_mx(out=codes[:].bitcast(FP8X4), scales=scales[:], in_=grp[:])
             return codes, scales
 
-        bbank = pv.tile([P, 512], F32, name="bbank", tag="pv")
+        bbank = banks.tile([P, 512], F32, name="bbank", tag="bank")
         nc.tensor.transpose(bbank[:, 0:P], btile[:].bitcast(F32), identf[:])
         bwords = const.tile([P, 8], F32, name="bwords")
         nc.vector.tensor_copy(out=bwords[:, 0:6], in_=bbank[:, 0:6])
@@ -131,60 +130,68 @@ def tile_rotelearningmemory_pa_t_kernel(
         nc.vector.tensor_scalar(out=nbg[:], in0=bias[:, 8:12], scalar1=-1.0, scalar2=None, op0=ALU.mult)
 
         weights = {}
-        SECTION = {"r": 0, "c": 1, "x": 2, "q": 3}
-        steps = {}
+        pairs = {}
 
         def ok(g):
             return 0 <= g < N_GROUPS
 
-        def step_of(g, key):
-            return g if key == "r" else g - 1
+        def home(g, key):
+            if key == "r" or key == "c":
+                name, bufs, half = ("rc", g if key == "r" else g - 2), 3, (0 if key == "r" else 1)
+            else:
+                name, bufs, half = ("xq", g), 5, (0 if key == "x" else 1)
+            if name not in pairs:
+                pairs[name] = {
+                    "grp": grps.tile(
+                        [P, 8 * GROUP], BF16, name="g%s%d" % (name[0], name[1] + 2), tag="g" + name[0], bufs=bufs,
+                        align_bytes=64,
+                    )
+                }
+            return pairs[name], half
 
         def grouped(g, key):
-            t = step_of(g, key)
-            if t not in steps:
-                steps[t] = {"grp": grps.tile([P, 16 * GROUP], BF16, name="grp%d" % (t + 1), tag="grp", align_bytes=64)}
-            first = SECTION[key] * 4 * GROUP
-            return steps[t]["grp"][:, first : first + 4 * GROUP]
+            pair, half = home(g, key)
+            return pair["grp"][:, half * 4 * GROUP : (half + 1) * 4 * GROUP]
 
-        def quantise_step(t):
-            if t < -1 or t >= N_GROUPS:
-                return
-            st = steps[t]
-            st["codes"] = cods.tile([P, 4 * GROUP], U32, name="codes%d" % (t + 1), tag="codes", align_bytes=64)
-            st["scales"] = cods.tile([P, 4 * GROUP], U8, name="scales%d" % (t + 1), tag="scales", align_bytes=64)
-            if t == -1:
-                spans = ((1, 2), (2, 4))
-            elif t == N_GROUPS - 1:
-                spans = ((0, 1),)
-            else:
-                spans = ((0, 4),)
-            for a, b in spans:
-                nc.vector.quantize_mx(
-                    out=st["codes"][:, a * GROUP : b * GROUP].bitcast(FP8X4),
-                    scales=st["scales"][:, a * GROUP : b * GROUP],
-                    in_=st["grp"][:, 4 * a * GROUP : 4 * b * GROUP],
-                )
+        def quantise(name, first, last):
+            pair = pairs[name]
+            label = "%s%d" % (name[0], name[1] + 2)
+            pair["codes"] = cods.tile([P, 2 * GROUP], U32, name="c" + label, tag="c" + name[0], align_bytes=64)
+            pair["scales"] = cods.tile([P, 2 * GROUP], U8, name="s" + label, tag="s" + name[0], align_bytes=64)
+            nc.vector.quantize_mx(
+                out=pair["codes"][:, first * GROUP : last * GROUP].bitcast(FP8X4),
+                scales=pair["scales"][:, first * GROUP : last * GROUP],
+                in_=pair["grp"][:, 4 * first * GROUP : 4 * last * GROUP],
+            )
+
+        def q_rc(t):
+            first = 0 if ok(t) else 1
+            last = 2 if ok(t + 2) else 1
+            if first < last:
+                quantise(("rc", t), first, last)
+
+        def q_xq(g):
+            if ok(g):
+                quantise(("xq", g), 0, 2)
 
         def ti(g, key):
             if not ok(g):
                 return
-            grp = grouped(g, key)
-            bank = ps.tile([P, 512], F32, name="ti%s%d" % (key, g), tag="ps")
+            bank = banks.tile([P, 512], F32, name="ti%s%d" % (key, g), tag="bank")
             transposes(bank, supers[g // 2][key], 2 * (g % 2), 0)
-            leave(False, grp.bitcast(F32).rearrange("p (n u) -> p n u", u=2), bank)
+            leave(False, grouped(g, key).bitcast(F32).rearrange("p (n u) -> p n u", u=2), bank)
 
         def mx(out, wkey, c, g, key, first, count, start, stop):
             wc, ws = weights[wkey]
-            st = steps[step_of(g, key)]
+            pair, half = home(g, key)
             col = slice(c * P, (c + 1) * P)
-            cols = slice(SECTION[key] * GROUP + first, SECTION[key] * GROUP + first + count)
+            cols = slice(half * GROUP + first, half * GROUP + first + count)
             nc.tensor.matmul_mx(
                 out=out,
                 lhsT=wc[:, col].bitcast(FP8X4),
                 lhsT_scale=ws[:, col],
-                rhs=st["codes"][:, cols].bitcast(FP8X4),
-                rhs_scale=st["scales"][:, cols],
+                rhs=pair["codes"][:, cols].bitcast(FP8X4),
+                rhs_scale=pair["scales"][:, cols],
                 start=start,
                 stop=stop,
             )
@@ -192,7 +199,7 @@ def tile_rotelearningmemory_pa_t_kernel(
         def m1(g, jj):
             if not ok(g):
                 return
-            bank = pv.tile([P, 512], F32, name="m1_%d_%d" % (g, jj), tag="pv")
+            bank = banks.tile([P, 512], F32, name="m1_%d_%d" % (g, jj), tag="bank")
             for c in range(4):
                 mx(bank[:, c * P : (c + 1) * P], "w1", c, g, "c", jj * P, P, True, True)
             nc.vector.tensor_tensor(
@@ -207,8 +214,8 @@ def tile_rotelearningmemory_pa_t_kernel(
                 return
             st = groups[g]
             if b == 0:
-                st["h"] = work.tile([P, 4, GROUP], F32, name="h%d" % g, tag="h")
-            bank = ps.tile([P, 512], F32, name="m3_%d_%d" % (g, b), tag="ps")
+                st["h"] = work.tile([P, 4, GROUP], F32, name="h%d" % g, tag="h", bufs=4)
+            bank = banks.tile([P, 512], F32, name="m3_%d_%d" % (g, b), tag="bank")
             for cc in range(2):
                 part = bank[:, cc * GROUP : (cc + 1) * GROUP]
                 mx(part, "wgx", 2 * b + cc, g, "x", 0, GROUP, True, False)
@@ -223,12 +230,18 @@ def tile_rotelearningmemory_pa_t_kernel(
         def m2(g, b):
             if not ok(g):
                 return
-            st = groups[g]
-            if b == 0:
-                st["dy"] = work.tile([P, 4, GROUP], F32, name="dy%d" % g, tag="dy")
-            bank = pv.tile([P, 512], F32, name="m2_%d_%d" % (g, b), tag="pv")
+            bank = banks.tile([P, 512], F32, name="m2_%d_%d" % (g, b), tag="bank")
+            groups[g]["m2_%d" % b] = bank
             for cc in range(2):
                 mx(bank[:, cc * GROUP : (cc + 1) * GROUP], "w2", 2 * b + cc, g, "r", 0, GROUP, True, True)
+
+        def sub(g, b):
+            if not ok(g):
+                return
+            st = groups[g]
+            if b == 0:
+                st["dy"] = work.tile([P, 4, GROUP], F32, name="dy%d" % g, tag="dy", bufs=4)
+            bank = st["m2_%d" % b]
             for cc in range(2):
                 c = 2 * b + cc
                 nc.vector.scalar_tensor_tensor(
@@ -255,7 +268,7 @@ def tile_rotelearningmemory_pa_t_kernel(
                 st["yc"] = work.tile([P, 2, WIDTH], F32, name="yc%d" % g, tag="yc")
                 for key in ("sums", "nmu", "ssq"):
                     st[key] = stat.tile([P, 2], F32, name="%s%d" % (key, g), tag=key)
-            bank = ps.tile([P, 512], F32, name="tb%d_%d" % (g, jj), tag="ps")
+            bank = banks.tile([P, 512], F32, name="tb%d_%d" % (g, jj), tag="bank")
             nc.tensor.matmul(
                 out=bank[:].rearrange("p (u e m) -> p u e m", u=2, e=2),
                 lhsT=identb[:],
@@ -279,11 +292,12 @@ def tile_rotelearningmemory_pa_t_kernel(
                 accum_out=st["sums"][:, jj : jj + 1],
             )
 
-        def mean(g):
+        def mean(g, jj):
             if not ok(g):
                 return
             st = groups[g]
-            nc.scalar.mul(out=st["nmu"][:], in_=st["sums"][:], mul=-1.0 / WIDTH)
+            one = slice(jj, jj + 1)
+            nc.scalar.mul(out=st["nmu"][:, one], in_=st["sums"][:, one], mul=-1.0 / WIDTH)
 
         def s2(g, jj):
             if not ok(g):
@@ -333,21 +347,16 @@ def tile_rotelearningmemory_pa_t_kernel(
                     in_=st["o"][:],
                 )
 
-        for t in range(-2, N_GROUPS + 3):
-            if t % 2 == 0 and 0 < (t + 4) // 2 < N_GROUPS // 2:
-                load((t + 4) // 2)
-            s2(t - 3, 0)
-            s2(t - 3, 1)
-            m1(t, 0)
-            m1(t, 1)
-            cm(t - 1, 0)
-            cm(t - 1, 1)
-            pw(t - 3)
-            ln1(t - 3, 0)
-            quantise_step(t)
-            ln1(t - 3, 1)
-            if t == -2:
+        loaded = 1
+        for t in range(-3, N_GROUPS + 4):
+            while loaded < N_GROUPS // 2 and 2 * loaded - 6 <= t:
+                load(loaded)
+                loaded += 1
+            if t == -3:
                 weights["w1"] = prepare_weight(w1raw, 0, "w1")
+            ln1(t - 4, 0)
+            q_rc(t)
+            ln1(t - 4, 1)
             if t == -1:
                 weights["wgx"] = prepare_weight(wgraw, 0, "wgx")
                 weights["wgq"] = prepare_weight(wgraw, 512, "wgq")
@@ -356,15 +365,26 @@ def tile_rotelearningmemory_pa_t_kernel(
             if t == 1:
                 nc.tensor.matmul(out=lnbank[:, 0:WIDTH], lhsT=identb[:], rhs=lng[:], start=True, stop=True)
                 nc.tensor.matmul(out=lnbank[:, WIDTH : 2 * WIDTH], lhsT=identb[:], rhs=lnb[:], start=True, stop=True)
-            ti(t + 2, "c")
-            tb(t - 2, 0)
+            ti(t + 3, "c")
+            tb(t - 3, 1)
+            mean(t - 3, 0)
             ti(t + 2, "x")
-            ln2(t - 3, 0)
-            ln2(t - 3, 1)
+            mean(t - 3, 1)
+            s2(t - 3, 0)
+            s2(t - 3, 1)
+            pw(t - 3)
+            m2(t - 1, 0)
+            m2(t - 1, 1)
             m3(t, 0)
             m3(t, 1)
-            m2(t, 0)
-            m2(t, 1)
-            tb(t - 2, 1)
+            sub(t - 1, 0)
+            sub(t - 1, 1)
+            cm(t - 1, 0)
+            cm(t - 1, 1)
+            ln2(t - 4, 0)
+            q_xq(t + 1)
+            ln2(t - 4, 1)
+            tb(t - 2, 0)
             ti(t + 2, "q")
-            mean(t - 2)
+            m1(t + 1, 0)
+            m1(t + 1, 1)

@@ -86,10 +86,12 @@ def tile_rotelearningmemory_pa_t_kernel(
         wgraw = load_weight(gate_w, 1024, "wgraw")
         w2raw = load_weight(op_w, 512, "w2raw")
 
-        lng = const.tile([P, WIDTH], BF16, name="lng")
-        nc.scalar.dma_start(out=lng[:], in_=ln_g.partition_broadcast(P))
-        lnb = const.tile([P, WIDTH], BF16, name="lnb")
-        nc.scalar.dma_start(out=lnb[:], in_=ln_b.partition_broadcast(P))
+        lnrow = const.tile([P, 2 * WIDTH], BF16, name="lnrow")
+        nc.vector.memset(lnrow[:], 0.0)
+        nc.scalar.dma_start(out=lnrow[0:1, 0:WIDTH], in_=ln_g.rearrange("(o d) -> o d", o=1))
+        nc.scalar.dma_start(out=lnrow[0:1, WIDTH : 2 * WIDTH], in_=ln_b.rearrange("(o d) -> o d", o=1))
+        ones = const.tile([P, P], BF16, name="ones")
+        nc.vector.memset(ones[:], 1.0)
         lnbank = pc.tile([P, 2 * WIDTH], BF16, name="lnbank")
 
         def transposes(bank, src, first, k0):
@@ -363,8 +365,10 @@ def tile_rotelearningmemory_pa_t_kernel(
             if t == 0:
                 weights["w2"] = prepare_weight(w2raw, 0, "w2")
             if t == 1:
-                nc.tensor.matmul(out=lnbank[:, 0:WIDTH], lhsT=identb[:], rhs=lng[:], start=True, stop=True)
-                nc.tensor.matmul(out=lnbank[:, WIDTH : 2 * WIDTH], lhsT=identb[:], rhs=lnb[:], start=True, stop=True)
+                nc.tensor.matmul(out=lnbank[:, 0:WIDTH], lhsT=ones[:], rhs=lnrow[:, 0:WIDTH], start=True, stop=True)
+                nc.tensor.matmul(
+                    out=lnbank[:, WIDTH : 2 * WIDTH], lhsT=ones[:], rhs=lnrow[:, WIDTH : 2 * WIDTH], start=True, stop=True
+                )
             ti(t + 3, "c")
             tb(t - 3, 1)
             mean(t - 3, 0)

@@ -357,8 +357,9 @@ def tile_rotelearningmemory_pa_t_kernel(
             if t == -3:
                 weights["w1"] = prepare_weight(w1raw, 0, "w1")
             ln1(t - 4, 0)
-            q_rc(t)
             ln1(t - 4, 1)
+            q_rc(t)
+            q_xq(t + 1)
             if t == -1:
                 weights["wgx"] = prepare_weight(wgraw, 0, "wgx")
                 weights["wgq"] = prepare_weight(wgraw, 512, "wgq")
@@ -386,7 +387,6 @@ def tile_rotelearningmemory_pa_t_kernel(
             cm(t - 1, 0)
             cm(t - 1, 1)
             ln2(t - 4, 0)
-            q_xq(t + 1)
             ln2(t - 4, 1)
             tb(t - 2, 0)
             ti(t + 2, "q")

@@ -356,10 +356,8 @@ def tile_rotelearningmemory_pa_t_kernel(
                 loaded += 1
             if t == -3:
                 weights["w1"] = prepare_weight(w1raw, 0, "w1")
-            ln1(t - 4, 0)
-            ln1(t - 4, 1)
-            q_rc(t)
             q_xq(t + 1)
+            q_rc(t)
             if t == -1:
                 weights["wgx"] = prepare_weight(wgraw, 0, "wgx")
                 weights["wgq"] = prepare_weight(wgraw, 512, "wgq")
@@ -388,6 +386,8 @@ def tile_rotelearningmemory_pa_t_kernel(
             cm(t - 1, 1)
             ln2(t - 4, 0)
             ln2(t - 4, 1)
+            ln1(t - 3, 0)
+            ln1(t - 3, 1)
             tb(t - 2, 0)
             ti(t + 2, "q")
             m1(t + 1, 0)

@@ -255,12 +255,12 @@ def tile_rotelearningmemory_pa_t_kernel(
                     op1=ALU.subtract,
                 )
 
-        def cm(g, jj):
+        def cm(g, b):
             if not ok(g):
                 return
             st = groups[g]
-            tok = slice(jj * P, (jj + 1) * P)
-            nc.gpsimd.tensor_tensor(out=st["dy"][:, :, tok], in0=st["dy"][:, :, tok], in1=st["h"][:, :, tok], op=ALU.mult)
+            two = slice(2 * b, 2 * b + 2)
+            nc.gpsimd.tensor_tensor(out=st["dy"][:, two, :], in0=st["dy"][:, two, :], in1=st["h"][:, two, :], op=ALU.mult)
 
         def tb(g, jj):
             if not ok(g):
@@ -356,8 +356,10 @@ def tile_rotelearningmemory_pa_t_kernel(
                 loaded += 1
             if t == -3:
                 weights["w1"] = prepare_weight(w1raw, 0, "w1")
-            q_xq(t + 1)
+            ln1(t - 4, 0)
+            ln1(t - 4, 1)
             q_rc(t)
+            q_xq(t + 1)
             if t == -1:
                 weights["wgx"] = prepare_weight(wgraw, 0, "wgx")
                 weights["wgq"] = prepare_weight(wgraw, 512, "wgq")
@@ -381,13 +383,11 @@ def tile_rotelearningmemory_pa_t_kernel(
             m3(t, 0)
             m3(t, 1)
             sub(t - 1, 0)
-            sub(t - 1, 1)
             cm(t - 1, 0)
+            sub(t - 1, 1)
             cm(t - 1, 1)
             ln2(t - 4, 0)
             ln2(t - 4, 1)
-            ln1(t - 3, 0)
-            ln1(t - 3, 1)
             tb(t - 2, 0)
             ti(t + 2, "q")
             m1(t + 1, 0)

from contextlib import ExitStack
import math

import concourse.mybir as mybir
from concourse.masks import make_identity

F32 = mybir.dt.float32
BF16 = mybir.dt.bfloat16
U32 = mybir.dt.uint32
U8 = mybir.dt.uint8
FP8X4 = mybir.dt.float8_e4m3fn_x4
ALU = mybir.AluOpType
ACT = mybir.ActivationFunctionType

P = 128
TOKENS = 4096
WIDTH = 512
GROUP = 256
SUPER = 512
N_GROUPS = TOKENS // GROUP
LN_EPS = 1e-5
FLOPS = 2 * TOKENS * WIDTH * (512 + 512 + 1024)

MANUAL = True


def tile_rotelearningmemory_pa_t_kernel(
    tc, x, query, ctx, attn_out_w, attn_out_b, op_w, op_b, gate_w, gate_b, ln_g, ln_b, out
):
    nc = tc.nc
    x_rows = x.flatten_outer_dims()
    q_rows = query.flatten_outer_dims()
    c_rows = ctx.flatten_outer_dims()
    o_rows = out.flatten_outer_dims()

    with ExitStack() as stack:
        if MANUAL:
            stack.enter_context(tc.manual_schedule())
        const = stack.enter_context(tc.tile_pool(name="const", bufs=1))
        wtmp = stack.enter_context(tc.tile_pool(name="wtmp", bufs=2))
        raws = stack.enter_context(tc.tile_pool(name="raws", bufs=3))
        grps = stack.enter_context(tc.tile_pool(name="grps", bufs=3))
        cods = stack.enter_context(tc.tile_pool(name="cods", bufs=3))
        work = stack.enter_context(tc.tile_pool(name="work", bufs=3))
        stat = stack.enter_context(tc.tile_pool(name="stat", bufs=4))
        pc = stack.enter_context(tc.psum_pool(name="pc", bufs=1))
        banks = stack.enter_context(tc.psum_pool(name="banks", bufs=7))

        identf = const.tile([P, P], F32, name="identf")
        make_identity(nc, identf[:])
        identb = const.tile([P, P], BF16, name="identb")
        make_identity(nc, identb[:])
        mhalf = const.tile([P, 2], F32, name="mhalf")
        nc.gpsimd.memset(mhalf[:], -0.5)
        btile = const.tile([P, 2 * P], BF16, name="btile")
        nc.vector.memset(btile[:], 0.0)
        junk = const.tile([P, WIDTH], BF16, name="junk")

        for v, vec in enumerate((attn_out_b, op_b, gate_b)):
            nc.scalar.dma_start(out=btile[2 * v : 2 * v + 2, :], in_=vec.rearrange("(u w) -> u w", u=2))

        def load_weight(w, cols, name):
            raw = const.tile([P, 4, cols], BF16, name=name)
            nc.sync.dma_start(
                out=raw[:].rearrange("m (u e) k -> m u (e k)", u=2),
                in_=w.rearrange("(u m e) k -> m u (e k)", u=2, e=2),
            )
            return raw

        supers = {}
        groups = {}
        for g in range(N_GROUPS):
            groups[g] = {}

        def load(s):
            st = {}
            supers[s] = st
            rows = slice(s * SUPER, (s + 1) * SUPER)
            for key, src, bufs in (("c", c_rows, 3), ("x", x_rows, 6), ("q", q_rows, 3)):
                raw = raws.tile([P, 4, WIDTH], BF16, name="raw%s%d" % (key, s), tag="raw" + key, bufs=bufs)
                nc.sync.dma_start(out=raw[:], in_=src[rows, :].rearrange("(p j) k -> p j k", j=4))
                st[key] = raw

        w1raw = load_weight(attn_out_w, 512, "w1raw")
        load(0)
        wgraw = load_weight(gate_w, 1024, "wgraw")
        w2raw = load_weight(op_w, 512, "w2raw")

        lnrow = const.tile([P, 2 * WIDTH], BF16, name="lnrow")
        nc.vector.memset(lnrow[:], 0.0)
        nc.scalar.dma_start(out=lnrow[0:1, 0:WIDTH], in_=ln_g.rearrange("(o d) -> o d", o=1))
        nc.scalar.dma_start(out=lnrow[0:1, WIDTH : 2 * WIDTH], in_=ln_b.rearrange("(o d) -> o d", o=1))
        ones = const.tile([P, P], BF16, name="ones")
        nc.vector.memset(ones[:], 1.0)
        lnbank = pc.tile([P, 2 * WIDTH], BF16, name="lnbank")

        def transposes(bank, src, first, k0):
            for jj in range(2):
                words = src[:, first + jj, k0 : k0 + 512].bitcast(F32)
                for u in range(2):
                    col = u * 256 + jj * P
                    nc.tensor.transpose(bank[:, col : col + P], words[:, u * P : (u + 1) * P], identf[:])

        def leave(on_vector, dst, bank):
            src = bank[:].rearrange("p (u n) -> p n u", u=2)
            if on_vector:
                nc.vector.tensor_copy(out=dst, in_=src)
            else:
                nc.scalar.copy(out=dst, in_=src)

        def words_of(grp):
            return grp[:].bitcast(F32).rearrange("p (n u) -> p n u", u=2)

        def prepare_weight(raw, k0, name):
            grp = wtmp.tile([P, 2048], BF16, name="g" + name, tag="wgrp", align_bytes=64)
            for half in range(2):
                bank = banks.tile([P, 512], F32, name="b%s%d" % (name, half), tag="bank")
                transposes(bank, raw, 2 * half, k0)
                leave(True, words_of(grp)[:, half * 256 : (half + 1) * 256, :], bank)
            codes = const.tile([P, 512], U32, name="c" + name, align_bytes=64)
            scales = const.tile([P, 512], U8, name="s" + name, align_bytes=64)
            nc.vector.quantize_mx(out=codes[:].bitcast(FP8X4), scales=scales[:], in_=grp[:])
            return codes, scales

        bbank = banks.tile([P, 512], F32, name="bbank", tag="bank")
        nc.tensor.transpose(bbank[:, 0:P], btile[:].bitcast(F32), identf[:])
        bwords = const.tile([P, 8], F32, name="bwords")
        nc.vector.tensor_copy(out=bwords[:, 0:6], in_=bbank[:, 0:6])
        bias = const.tile([P, 12], F32, name="bias")
        nc.vector.tensor_copy(out=bias[:], in_=bwords[:, 0:6].bitcast(BF16))
        nbg = const.tile([P, 4], F32, name="nbg")
        nc.vector.tensor_scalar(out=nbg[:], in0=bias[:, 8:12], scalar1=-1.0, scalar2=None, op0=ALU.mult)

        weights = {}
        pairs = {}

        def ok(g):
            return 0 <= g < N_GROUPS

        def home(g, key):
            if key == "r" or key == "c":
                name, bufs, half = ("rc", g if key == "r" else g - 2), 3, (0 if key == "r" else 1)
            else:
                name, bufs, half = ("xq", g), 5, (0 if key == "x" else 1)
            if name not in pairs:
                pairs[name] = {
                    "grp": grps.tile(
                        [P, 8 * GROUP], BF16, name="g%s%d" % (name[0], name[1] + 2), tag="g" + name[0], bufs=bufs,
                        align_bytes=64,
                    )
                }
            return pairs[name], half

        def grouped(g, key):
            pair, half = home(g, key)
            return pair["grp"][:, half * 4 * GROUP : (half + 1) * 4 * GROUP]

        def quantise(name, first, last):
            pair = pairs[name]
            label = "%s%d" % (name[0], name[1] + 2)
            pair["codes"] = cods.tile([P, 2 * GROUP], U32, name="c" + label, tag="c" + name[0], align_bytes=64)
            pair["scales"] = cods.tile([P, 2 * GROUP], U8, name="s" + label, tag="s" + name[0], align_bytes=64)
            nc.vector.quantize_mx(
                out=pair["codes"][:, first * GROUP : last * GROUP].bitcast(FP8X4),
                scales=pair["scales"][:, first * GROUP : last * GROUP],
                in_=pair["grp"][:, 4 * first * GROUP : 4 * last * GROUP],
            )

        def q_rc(t):
            first = 0 if ok(t) else 1
            last = 2 if ok(t + 2) else 1
            if first < last:
                quantise(("rc", t), first, last)

        def q_xq(g):
            if ok(g):
                quantise(("xq", g), 0, 2)

        def ti(g, key):
            if not ok(g):
                return
            bank = banks.tile([P, 512], F32, name="ti%s%d" % (key, g), tag="bank")
            transposes(bank, supers[g // 2][key], 2 * (g % 2), 0)
            leave(False, grouped(g, key).bitcast(F32).rearrange("p (n u) -> p n u", u=2), bank)

        def mx(out, wkey, c, g, key, first, count, start, stop):
            wc, ws = weights[wkey]
            pair, half = home(g, key)
            col = slice(c * P, (c + 1) * P)
            cols = slice(half * GROUP + first, half * GROUP + first + count)
            nc.tensor.matmul_mx(
                out=out,
                lhsT=wc[:, col].bitcast(FP8X4),
                lhsT_scale=ws[:, col],
                rhs=pair["codes"][:, cols].bitcast(FP8X4),
                rhs_scale=pair["scales"][:, cols],
                start=start,
                stop=stop,
            )

        def m1(g, jj):
            if not ok(g):
                return
            bank = banks.tile([P, 512], F32, name="m1_%d_%d" % (g, jj), tag="bank")
            for c in range(4):
                mx(bank[:, c * P : (c + 1) * P], "w1", c, g, "c", jj * P, P, True, True)
            nc.vector.tensor_tensor(
                out=grouped(g, "r").rearrange("p (n c) -> p n c", c=4)[:, jj * P : (jj + 1) * P, :],
                in0=bank[:].rearrange("p (c n) -> p n c", c=4),
                in1=bias[:, 0:4].unsqueeze(1).to_broadcast([P, P, 4]),
                op=ALU.add,
            )

        def m3(g, b):
            if not ok(g):
                return
            st = groups[g]
            if b == 0:
                st["h"] = work.tile([P, 4, GROUP], F32, name="h%d" % g, tag="h", bufs=4)
            bank = banks.tile([P, 512], F32, name="m3_%d_%d" % (g, b), tag="bank")
            for cc in range(2):
                part = bank[:, cc * GROUP : (cc + 1) * GROUP]
                mx(part, "wgx", 2 * b + cc, g, "x", 0, GROUP, True, False)
                mx(part, "wgq", 2 * b + cc, g, "q", 0, GROUP, False, True)
            for cc in range(2):
                c = 2 * b + cc
                nc.scalar.activation(
                    out=st["h"][:, c, :], in_=bank[:, cc * GROUP : (cc + 1) * GROUP], func=ACT.Sigmoid,
                    bias=nbg[:, c : c + 1], scale=-1.0,
                )

        def m2(g, b):
            if not ok(g):
                return
            bank = banks.tile([P, 512], F32, name="m2_%d_%d" % (g, b), tag="bank")
            groups[g]["m2_%d" % b] = bank
            for cc in range(2):
                mx(bank[:, cc * GROUP : (cc + 1) * GROUP], "w2", 2 * b + cc, g, "r", 0, GROUP, True, True)

        def sub(g, b):
            if not ok(g):
                return
            st = groups[g]
            if b == 0:
                st["dy"] = work.tile([P, 4, GROUP], F32, name="dy%d" % g, tag="dy", bufs=4)
            bank = st["m2_%d" % b]
            for cc in range(2):
                c = 2 * b + cc
                nc.vector.scalar_tensor_tensor(
                    out=st["dy"][:, c, :],
                    in0=bank[:, cc * GROUP : (cc + 1) * GROUP],
                    scalar=bias[:, 4 + c : 5 + c],
                    in1=grouped(g, "x").rearrange("p (n t) -> p n t", t=4)[:, :, c],
                    op0=ALU.add,
                    op1=ALU.subtract,
                )

        def cm(g, b):
            if not ok(g):
                return
            st = groups[g]
            two = slice(2 * b, 2 * b + 2)
            nc.gpsimd.tensor_tensor(out=st["dy"][:, two, :], in0=st["dy"][:, two, :], in1=st["h"][:, two, :], op=ALU.mult)

        def tb(g, jj):
            if not ok(g):
                return
            st = groups[g]
            if jj == 0:
                st["yc"] = work.tile([P, 2, WIDTH], F32, name="yc%d" % g, tag="yc")
                for key in ("sums", "nmu", "ssq"):
                    st[key] = stat.tile([P, 2], F32, name="%s%d" % (key, g), tag=key)
            bank = banks.tile([P, 512], F32, name="tb%d_%d" % (g, jj), tag="bank")
            nc.tensor.matmul(
                out=bank[:].rearrange("p (u e m) -> p u e m", u=2, e=2),
                lhsT=identb[:],
                rhs=supers[g // 2]["x"][:, 2 * (g % 2) + jj, :].rearrange("p (u m e) -> p u e m", u=2, e=2),
                start=True,
                stop=False,
            )
            for c in range(4):
                nc.tensor.matmul(
                    out=bank[:, c * P : (c + 1) * P],
                    lhsT=st["dy"][:, c, jj * P : (jj + 1) * P],
                    rhs=identf[:],
                    is_transpose=True,
                    start=False,
                    stop=(c == 3),
                )
            nc.scalar.activation(
                out=st["yc"][:, jj, :].rearrange("p (u m e) -> p u m e", u=2, e=2),
                in_=bank[:].rearrange("p (u e m) -> p u m e", u=2, e=2),
                func=ACT.Identity,
                accum_out=st["sums"][:, jj : jj + 1],
            )

        def mean(g, jj):
            if not ok(g):
                return
            st = groups[g]
            one = slice(jj, jj + 1)
            nc.scalar.mul(out=st["nmu"][:, one], in_=st["sums"][:, one], mul=-1.0 / WIDTH)

        def s2(g, jj):
            if not ok(g):
                return
            st = groups[g]
            one = slice(jj, jj + 1)
            nc.scalar.activation(
                out=junk[:], in_=st["yc"][:, jj, :], func=ACT.Square, bias=st["nmu"][:, one], scale=1.0,
                accum_out=st["ssq"][:, one],
            )

        def pw(g):
            if not ok(g):
                return
            st = groups[g]
            st["var"] = stat.tile([P, 2], F32, name="var%d" % g, tag="var")
            st["rs"] = stat.tile([P, 2], F32, name="rs%d" % g, tag="rs")
            nc.gpsimd.tensor_scalar(
                out=st["var"][:], in0=st["ssq"][:], scalar1=1.0 / WIDTH, scalar2=LN_EPS, op0=ALU.mult, op1=ALU.add
            )
            nc.gpsimd.tensor_tensor(out=st["rs"][:], in0=st["var"][:], in1=mhalf[:], op=ALU.pow)

        def ln1(g, jj):
            if not ok(g):
                return
            st = groups[g]
            if jj == 0:
                st["o"] = work.tile([P, 2, WIDTH], F32, name="o%d" % g, tag="o")
            nc.vector.scalar_tensor_tensor(
                out=st["o"][:, jj, :], in0=st["yc"][:, jj, :], scalar=st["nmu"][:, jj : jj + 1], in1=lnbank[:, 0:WIDTH],
                op0=ALU.add, op1=ALU.mult,
            )

        def ln2(g, jj):
            if not ok(g):
                return
            st = groups[g]
            nc.vector.scalar_tensor_tensor(
                out=st["o"][:, jj, :], in0=st["o"][:, jj, :], scalar=st["rs"][:, jj : jj + 1],
                in1=lnbank[:, WIDTH : 2 * WIDTH], op0=ALU.mult, op1=ALU.add,
            )
            if jj == 1:
                s = g // 2
                first = 2 * (g % 2)
                nc.sync.dma_start(
                    out=o_rows[s * SUPER : (s + 1) * SUPER, :].rearrange("(p j) d -> p j d", j=4)[:, first : first + 2, :],
                    in_=st["o"][:],
                )

        loaded = 1
        for t in range(-3, N_GROUPS + 4):
            while loaded < N_GROUPS // 2 and 2 * loaded - 6 <= t:
                load(loaded)
                loaded += 1
            if t == -3:
                weights["w1"] = prepare_weight(w1raw, 0, "w1")
            ln1(t - 4, 0)
            ln1(t - 4, 1)
            q_rc(t)
            q_xq(t + 1)
            if t == -1:
                weights["wgx"] = prepare_weight(wgraw, 0, "wgx")
                weights["wgq"] = prepare_weight(wgraw, 512, "wgq")
            if t == 0:
                weights["w2"] = prepare_weight(w2raw, 0, "w2")
            if t == 1:
                nc.tensor.matmul(out=lnbank[:, 0:WIDTH], lhsT=ones[:], rhs=lnrow[:, 0:WIDTH], start=True, stop=True)
                nc.tensor.matmul(
                    out=lnbank[:, WIDTH : 2 * WIDTH], lhsT=ones[:], rhs=lnrow[:, WIDTH : 2 * WIDTH], start=True, stop=True
                )
            ti(t + 3, "c")
            tb(t - 3, 1)
            mean(t - 3, 0)
            ti(t + 2, "x")
            mean(t - 3, 1)
            s2(t - 3, 0)
            s2(t - 3, 1)
            pw(t - 3)
            m2(t - 1, 0)
            m2(t - 1, 1)
            m3(t, 0)
            m3(t, 1)
            sub(t - 1, 0)
            cm(t - 1, 0)
            sub(t - 1, 1)
            cm(t - 1, 1)
            ln2(t - 4, 0)
            ln2(t - 4, 1)
            tb(t - 2, 0)
            ti(t + 2, "q")
            m1(t + 1, 0)
            m1(t + 1, 1)
